import numpy as np
import ml_dtypes


def mxq(x, axis, fmt="e4m3"):
    dtype, down = {"e4m3": (ml_dtypes.float8_e4m3fn, 7), "e5m2": (ml_dtypes.float8_e5m2, 14)}[fmt]
    v = np.moveaxis(np.asarray(x, np.float32).astype(ml_dtypes.bfloat16).astype(np.float64), axis, -1)
    blocks = v.reshape(v.shape[:-1] + (-1, 32))
    amax = np.abs(blocks).max(-1, keepdims=True)
    byte = np.maximum(np.where(amax > 0, np.frexp(amax)[1] - 1 + 127, 0) - down, 1)
    scale = np.exp2(byte - 127.0)
    codes = (blocks / scale).astype(np.float32).astype(dtype).astype(np.float64)
    return np.moveaxis((codes * scale).reshape(v.shape), -1, axis)


WIDE = False


def mx_kscale(k):
    if not WIDE:
        return np.ones(k)
    levels = np.array([10, -10, 5, -5, 0])
    if k % 512:
        return np.exp2(np.random.permutation(np.resize(levels, k // 32))).repeat(32)
    a = np.empty((k // 512, 16))
    for p in range(k // 512):
        a[p, :8] = np.random.permutation(np.resize(levels, 8))
        for g in range(8):
            far = levels[np.abs(levels - a[p, g]) >= 10]
            a[p, g + 8] = far[np.random.randint(len(far))]
    return np.exp2(a.ravel()).repeat(32)


BF16 = ml_dtypes.bfloat16


def bf(x):
    return np.asarray(x, np.float32).astype(BF16)


def f64(x):
    return np.asarray(x).astype(np.float64)


B, CIN, CM, CO, H, WD = 1, 512, 512, 512, 16, 16
RING = [(-1, -1), (-1, 0), (-1, 1), (0, 1), (1, 1), (1, 0), (1, -1), (0, -1)]
NUM_K = 9
KERNEL_ROT = 4
STEP = 2
M = NUM_K * CM


def setup_inputs():
    s = mx_kscale(CIN)
    t = mx_kscale(CM)
    return {"x": bf(np.random.standard_normal((B, CIN, H, WD)) * s[None, :, None, None]),
            "W": bf(np.random.standard_normal((CM, CIN, NUM_K)) / np.sqrt(CIN) / s[None, :, None] * t[:, None, None]),
            "W1": bf(np.random.standard_normal((CO, M)) * 1.4 / np.sqrt(M) / np.tile(t, NUM_K)[None, :])}


def reference(x, W, W1):
    xq = mxq(f64(x), 1, "e4m3")
    Wq = mxq(f64(W), 1, "e4m3")
    z = (Wq.transpose(0, 2, 1).reshape(CM * NUM_K, CIN) @ xq.reshape(B, CIN, H * WD)).reshape(B, CM, NUM_K, H, WD)
    h = np.maximum(z, 0.0)
    hq = mxq(h, 1, "e4m3")
    W1q = mxq(f64(W1).reshape(CO, NUM_K, CM), 2, "e4m3")
    u = (W1q.transpose(1, 0, 2) @ hq.transpose(0, 2, 1, 3, 4).reshape(B, NUM_K, CM, H * WD)).reshape(B, NUM_K, CO, H, WD)
    up = np.pad(u, ((0, 0), (0, 0), (0, 0), (1, 1), (1, 1)))
    rot_out = []
    for rot in range(KERNEL_ROT):
        roff = STEP * rot
        acc = 0.0
        for k in range(NUM_K):
            dy, dx = (0, 0) if k == NUM_K - 1 else RING[(k + roff) % len(RING)]
            acc = acc + up[:, k, :, 1 + dy:1 + dy + H, 1 + dx:1 + dx + WD]
        rot_out.append(acc)
    return np.stack(rot_out, axis=2)

@@ -1,0 +1,251 @@
+from contextlib import ExitStack
+
+import concourse.mybir as mybir
+from concourse.masks import make_identity
+
+F32 = mybir.dt.float32
+BF16 = mybir.dt.bfloat16
+U32 = mybir.dt.uint32
+U8 = mybir.dt.uint8
+FP8X4 = mybir.dt.float8_e4m3fn_x4
+RELU = mybir.ActivationFunctionType.Relu
+
+P = 128
+NK = 9
+HW = 256
+ROW = 64
+RING = [(-1, -1), (-1, 0), (-1, 1), (0, 1), (1, 1), (1, 0), (1, -1), (0, -1)]
+NSET = 3
+N_WARM = 10
+Z_DT = F32
+
+FLOPS = 2 * 2 * NK * 512 * 512 * HW
+
+
+def tile_psr4convf_kernel(tc, x, W, W1, out):
+    nc = tc.nc
+    x_v = x[0].rearrange("(p j) h w -> p j (h w)", j=4)
+    w_v = W.rearrange("(m t) c k -> m t (c k)", t=4)
+    w1_v = W1.rearrange("(m q) f -> m q f", q=4)
+    out_v = out[0].rearrange("(m q) r h w -> m q (r h w)", q=4)
+
+    with ExitStack() as ctx:
+        const = ctx.enter_context(tc.tile_pool(name="const", bufs=1))
+        raw = ctx.enter_context(tc.tile_pool(name="raw", bufs=6))
+        stage = ctx.enter_context(tc.tile_pool(name="stage", bufs=3))
+        outp = ctx.enter_context(tc.tile_pool(name="outp", bufs=4))
+
+        wraw = []
+        for t in range(4):
+            r = raw.tile([P, NK * 512], BF16, name="wraw%d" % t, tag="raw")
+            nc.sync.dma_start(out=r[:], in_=w_v[:, t, :])
+            wraw.append(r)
+        xraw = const.tile([P, 4, HW], BF16, name="xraw")
+        nc.sync.dma_start(out=xraw[:], in_=x_v)
+        w1raw = []
+
+        def load_w1(q):
+            r1 = raw.tile([P, NK * 512], BF16, name="w1raw%d" % q, tag="raw")
+            nc.sync.dma_start(out=r1[:], in_=w1_v[:, q, :])
+            w1raw.append(r1)
+
+        load_w1(0)
+        load_w1(1)
+
+        ident_bf = const.tile([P, P], BF16, name="ident_bf")
+        make_identity(nc, ident_bf[:])
+        ident_f = const.tile([P, P], F32, name="ident_f")
+        make_identity(nc, ident_f[:])
+        dummy = const.tile([P, 512], BF16, name="dummy")
+        nc.vector.memset(dummy[:], 0.0)
+        hset = []
+        for s in range(NSET):
+            trio = []
+            for nm in ("h0", "hp", "hm"):
+                ht = const.tile([P, 18, 16, 4], BF16, name="%s_%d" % (nm, s), align_bytes=64)
+                nc.vector.memset(ht[:], 0.0)
+                trio.append(ht)
+            hset.append(trio)
+        warm = const.tile([P, 1], F32, name="warm")
+        nc.vector.memset(warm[:], 0.0)
+        nc.scalar.activation(out=warm[:], in_=warm[:], func=RELU)
+
+        xg = const.tile([P, HW, 4], BF16, name="xg", align_bytes=64)
+        nc.vector.tensor_copy(out=xg[:], in_=xraw[:].rearrange("p j n -> p n j"))
+        xc = const.tile([P, HW], U32, name="xc", align_bytes=64)
+        xs = const.tile([P, HW], U8, name="xs", align_bytes=64)
+        nc.vector.quantize_mx(out=xc[:].bitcast(FP8X4), scales=xs[:], in_=xg[:].rearrange("p n j -> p (n j)"))
+
+        wc = const.tile([P, 4 * NK * P], U32, name="wc", align_bytes=64)
+        ws = const.tile([P, 4 * NK * P], U8, name="ws", align_bytes=64)
+        w1c = const.tile([P, 4 * NK * P], U32, name="w1c", align_bytes=64)
+        w1s = const.tile([P, 4 * NK * P], U8, name="w1s", align_bytes=64)
+        hc = []
+        hs = []
+        for k in range(NK):
+            nver = 4 if k < 8 else 2
+            hck = const.tile([P, nver * HW], U32, name="hc%d" % k, align_bytes=64)
+            hsk = const.tile([P, nver * HW], U8, name="hs%d" % k, align_bytes=64)
+            hc.append(hck)
+            hs.append(hsk)
+
+        def quantize_piece(grouped, codes, scales, chunk, k0, k1):
+            c0 = (chunk * NK + k0) * P
+            c1 = (chunk * NK + k1) * P
+            nc.vector.quantize_mx(
+                out=codes[:, c0:c1].bitcast(FP8X4),
+                scales=scales[:, c0:c1],
+                in_=grouped[:, k0 * 512 : k1 * 512],
+            )
+
+        work = ctx.enter_context(tc.psum_pool(name="work", bufs=4))
+        accp = ctx.enter_context(tc.psum_pool(name="accp", bufs=4))
+
+        def w_chunk(t):
+            wg = stage.tile([P, NK * 512], BF16, name="wg", tag="grouped", align_bytes=64)
+            src = wraw[t][:].rearrange("m (a j k) -> m j k a", j=4, k=NK)
+            for k in range(NK):
+                tp = work.tile([P, 4, P], BF16, name="tpw", tag="bank")
+                for j in range(4):
+                    nc.tensor.transpose(out=tp[:, j, :], in_=src[:, j, k, :], identity=ident_bf[:])
+                dst = wg[:, k * 512 : (k + 1) * 512].rearrange("p (m j) -> p m j", j=4)
+                if k % 2 == 0:
+                    nc.scalar.copy(out=dst, in_=tp[:].rearrange("p j m -> p m j"))
+                else:
+                    nc.vector.tensor_copy(out=dst, in_=tp[:].rearrange("p j m -> p m j"))
+                if k == 4:
+                    quantize_piece(wg, wc, ws, t, 0, 4)
+                if k == 8:
+                    quantize_piece(wg, wc, ws, t, 4, 8)
+            quantize_piece(wg, wc, ws, t, 8, 9)
+
+        def w1_chunk(q):
+            w1g = stage.tile([P, NK * 512], BF16, name="w1g", tag="grouped", align_bytes=64)
+            words = w1raw[q][:].bitcast(F32).rearrange("m (k a u) -> m k u a", k=NK, u=2)
+            for k0 in range(0, NK, 2):
+                nk = min(2, NK - k0)
+                tp1 = work.tile([P, 2, 2, P], F32, name="tp1", tag="bank")
+                for kk in range(nk):
+                    for u in range(2):
+                        nc.tensor.transpose(out=tp1[:, kk, u, :], in_=words[:, k0 + kk, u, :], identity=ident_f[:])
+                dst = (
+                    w1g[:, k0 * 512 : (k0 + nk) * 512]
+                    .bitcast(F32)
+                    .rearrange("p (k m u) -> p k m u", k=nk, u=2)
+                )
+                nc.scalar.copy(out=dst, in_=tp1[:, 0:nk, :, :].rearrange("p k u m -> p k m u"))
+                if k0 == 4:
+                    quantize_piece(w1g, w1c, w1s, q, 0, 4)
+                if k0 == 8:
+                    quantize_piece(w1g, w1c, w1s, q, 4, 8)
+            quantize_piece(w1g, w1c, w1s, q, 8, 9)
+
+        def stage1(k):
+            h0, hp, hm = hset[k % NSET]
+            h0f = h0[:].rearrange("p a b t -> p (a b t)")
+            for nh in range(2):
+                z = work.tile([P, 4, P], Z_DT, name="z", tag="bank")
+                for t in range(4):
+                    c0 = (t * NK + k) * P
+                    nc.tensor.matmul_mx(
+                        out=z[:, t, :],
+                        lhsT=wc[:, c0 : c0 + P].bitcast(FP8X4),
+                        lhsT_scale=ws[:, c0 : c0 + P],
+                        rhs=xc[:, nh * P : (nh + 1) * P].bitcast(FP8X4),
+                        rhs_scale=xs[:, nh * P : (nh + 1) * P],
+                        start=True,
+                        stop=True,
+                    )
+                nc.scalar.activation(
+                    out=h0f[:, ROW + nh * 512 : ROW + (nh + 1) * 512].rearrange("p (n t) -> p n t", t=4),
+                    in_=z[:].rearrange("p t n -> p n t"),
+                    func=RELU,
+                )
+            if k < 8:
+                nc.vector.tensor_copy(out=hp[:, 1:17, 0:15, :], in_=h0[:, 1:17, 1:16, :])
+                if k % 2 == 1:
+                    nc.scalar.copy(out=hm[:, 1:17, 1:16, :], in_=h0[:, 1:17, 0:15, :])
+                else:
+                    nc.vector.tensor_copy(out=hm[:, 1:17, 1:16, :], in_=h0[:, 1:17, 0:15, :])
+
+        def versions(k):
+            h0, hp, hm = hset[k % NSET]
+            by_dx = {0: h0, 1: hp, -1: hm}
+            for v in range(4 if k < 8 else 2):
+                dy, dx = RING[(k + 2 * v) % 8] if k < 8 else (0, 0)
+                flat = by_dx[dx][:].rearrange("p a b t -> p (a b t)")
+                nc.vector.quantize_mx(
+                    out=hc[k][:, v * HW : (v + 1) * HW].bitcast(FP8X4),
+                    scales=hs[k][:, v * HW : (v + 1) * HW],
+                    in_=flat[:, (1 + dy) * ROW : (1 + dy) * ROW + 4 * HW],
+                )
+
+        accs = {}
+
+        def open_group(q, rp):
+            acc = accp.tile([P, 512], F32, name="acc", tag="acc")
+            accs[(q, rp)] = acc
+
+        def stage2(q, rp, k, first_pass, last_pass):
+            c0 = (q * NK + k) * P
+            r0 = rp * 512 if k < 8 else 0
+            nc.tensor.matmul_mx(
+                out=accs[(q, rp)][:],
+                lhsT=w1c[:, c0 : c0 + P].bitcast(FP8X4),
+                lhsT_scale=w1s[:, c0 : c0 + P],
+                rhs=hc[k][:, r0 : r0 + 512].bitcast(FP8X4),
+                rhs_scale=hs[k][:, r0 : r0 + 512],
+                start=first_pass,
+                stop=last_pass,
+            )
+
+        def finish_group(q, rp):
+            osb = outp.tile([P, 512], F32, name="osb", tag="osb")
+            if rp == 0:
+                nc.vector.tensor_copy(out=osb[:], in_=accs[(q, rp)][:])
+            else:
+                nc.scalar.copy(out=osb[:], in_=accs[(q, rp)][:])
+            nc.sync.dma_start(out=out_v[:, q, rp * 512 : (rp + 1) * 512], in_=osb[:])
+
+        ks = [8, 0, 1, 2, 3, 4, 5, 6, 7]
+        first = [(q, rp) for q in (0, 1) for rp in (0, 1)]
+
+        def whole_group(q, rp):
+            open_group(q, rp)
+            for k in range(NK):
+                stage2(q, rp, k, k == 0, k == NK - 1)
+            finish_group(q, rp)
+
+        with tc.manual_schedule(engines={mybir.EngineType.PE}):
+            wps = work.tile([P, 512], F32, name="wps", tag="bank")
+            for i in range(N_WARM):
+                nc.tensor.matmul(out=wps[:], lhsT=dummy[:, 0:P], rhs=dummy[:], start=True, stop=True)
+            w_chunk(0)
+            load_w1(2)
+            w_chunk(1)
+            load_w1(3)
+            w_chunk(2)
+            w_chunk(3)
+            w1_chunk(0)
+            for g in first:
+                open_group(g[0], g[1])
+            for s in range(NK):
+                stage1(ks[s])
+                if s >= 1:
+                    versions(ks[s - 1])
+                if s == 1:
+                    w1_chunk(1)
+                if s >= 2:
+                    for g in first:
+                        stage2(g[0], g[1], ks[s - 2], s == 2, False)
+            versions(ks[NK - 1])
+            w1_chunk(2)
+            for g in first:
+                stage2(g[0], g[1], ks[NK - 2], False, False)
+                stage2(g[0], g[1], ks[NK - 1], False, True)
+                finish_group(g[0], g[1])
+            whole_group(2, 0)
+            w1_chunk(3)
+            whole_group(2, 1)
+            whole_group(3, 0)
+            whole_group(3, 1)

@@ -9,6 +9,7 @@ U32 = mybir.dt.uint32
 U8 = mybir.dt.uint8
 FP8X4 = mybir.dt.float8_e4m3fn_x4
 RELU = mybir.ActivationFunctionType.Relu
+ADD = mybir.AluOpType.add
 
 P = 128
 NK = 9
@@ -16,8 +17,10 @@ HW = 256
 ROW = 64
 RING = [(-1, -1), (-1, 0), (-1, 1), (0, 1), (1, 1), (1, 0), (1, -1), (0, -1)]
 NSET = 3
-N_WARM = 10
+N_WARM = 6
 Z_DT = F32
+C_RUNS = {"a": [(0, 2), (2, 2), (4, 1)], "b": [(5, 2), (7, 2)]}
+C_PIECES = {"a": [(0, 4), (4, 5)], "b": [(5, 9)]}
 
 FLOPS = 2 * 2 * NK * 512 * 512 * HW
 
@@ -31,9 +34,11 @@ def tile_psr4convf_kernel(tc, x, W, W1, out):
 
     with ExitStack() as ctx:
         const = ctx.enter_context(tc.tile_pool(name="const", bufs=1))
-        raw = ctx.enter_context(tc.tile_pool(name="raw", bufs=6))
-        stage = ctx.enter_context(tc.tile_pool(name="stage", bufs=3))
+        raw = ctx.enter_context(tc.tile_pool(name="raw", bufs=5))
+        stage = ctx.enter_context(tc.tile_pool(name="stage", bufs=5))
         outp = ctx.enter_context(tc.tile_pool(name="outp", bufs=4))
+        work = ctx.enter_context(tc.psum_pool(name="work", bufs=4))
+        accp = ctx.enter_context(tc.psum_pool(name="accp", bufs=4))
 
         wraw = []
         for t in range(4):
@@ -50,14 +55,13 @@ def tile_psr4convf_kernel(tc, x, W, W1, out):
             w1raw.append(r1)
 
         load_w1(0)
-        load_w1(1)
 
+        dummy = const.tile([P, 512], BF16, name="dummy")
+        nc.vector.memset(dummy[:], 0.0)
         ident_bf = const.tile([P, P], BF16, name="ident_bf")
         make_identity(nc, ident_bf[:])
         ident_f = const.tile([P, P], F32, name="ident_f")
         make_identity(nc, ident_f[:])
-        dummy = const.tile([P, 512], BF16, name="dummy")
-        nc.vector.memset(dummy[:], 0.0)
         hset = []
         for s in range(NSET):
             trio = []
@@ -71,11 +75,8 @@ def tile_psr4convf_kernel(tc, x, W, W1, out):
         nc.scalar.activation(out=warm[:], in_=warm[:], func=RELU)
 
         xg = const.tile([P, HW, 4], BF16, name="xg", align_bytes=64)
-        nc.vector.tensor_copy(out=xg[:], in_=xraw[:].rearrange("p j n -> p n j"))
         xc = const.tile([P, HW], U32, name="xc", align_bytes=64)
         xs = const.tile([P, HW], U8, name="xs", align_bytes=64)
-        nc.vector.quantize_mx(out=xc[:].bitcast(FP8X4), scales=xs[:], in_=xg[:].rearrange("p n j -> p (n j)"))
-
         wc = const.tile([P, 4 * NK * P], U32, name="wc", align_bytes=64)
         ws = const.tile([P, 4 * NK * P], U8, name="ws", align_bytes=64)
         w1c = const.tile([P, 4 * NK * P], U32, name="w1c", align_bytes=64)
@@ -83,11 +84,15 @@ def tile_psr4convf_kernel(tc, x, W, W1, out):
         hc = []
         hs = []
         for k in range(NK):
-            nver = 4 if k < 8 else 2
+            nver = 4 if k < 8 else 1
             hck = const.tile([P, nver * HW], U32, name="hc%d" % k, align_bytes=64)
             hsk = const.tile([P, nver * HW], U8, name="hs%d" % k, align_bytes=64)
             hc.append(hck)
             hs.append(hsk)
+
+        def x_prep():
+            nc.vector.tensor_copy(out=xg[:], in_=xraw[:].rearrange("p j n -> p n j"))
+            nc.vector.quantize_mx(out=xc[:].bitcast(FP8X4), scales=xs[:], in_=xg[:].rearrange("p n j -> p (n j)"))
 
         def quantize_piece(grouped, codes, scales, chunk, k0, k1):
             c0 = (chunk * NK + k0) * P
@@ -98,11 +103,16 @@ def tile_psr4convf_kernel(tc, x, W, W1, out):
                 in_=grouped[:, k0 * 512 : k1 * 512],
             )
 
-        work = ctx.enter_context(tc.psum_pool(name="work", bufs=4))
-        accp = ctx.enter_context(tc.psum_pool(name="accp", bufs=4))
+        def burst(n, lhs, rhs):
+            wps = work.tile([P, 512], F32, name="wps", tag="bank")
+            for i in range(n):
+                nc.tensor.matmul(out=wps[:], lhsT=lhs, rhs=rhs, start=True, stop=True)
 
-        def w_chunk(t):
+        wgs = {}
+
+        def w_tiles(t):
             wg = stage.tile([P, NK * 512], BF16, name="wg", tag="grouped", align_bytes=64)
+            wgs[t] = wg
             src = wraw[t][:].rearrange("m (a j k) -> m j k a", j=4, k=NK)
             for k in range(NK):
                 tp = work.tile([P, 4, P], BF16, name="tpw", tag="bank")
@@ -113,17 +123,21 @@ def tile_psr4convf_kernel(tc, x, W, W1, out):
                     nc.scalar.copy(out=dst, in_=tp[:].rearrange("p j m -> p m j"))
                 else:
                     nc.vector.tensor_copy(out=dst, in_=tp[:].rearrange("p j m -> p m j"))
-                if k == 4:
-                    quantize_piece(wg, wc, ws, t, 0, 4)
-                if k == 8:
-                    quantize_piece(wg, wc, ws, t, 4, 8)
-            quantize_piece(wg, wc, ws, t, 8, 9)
 
-        def w1_chunk(q):
-            w1g = stage.tile([P, NK * 512], BF16, name="w1g", tag="grouped", align_bytes=64)
+        def w_quant(t):
+            quantize_piece(wgs[t], wc, ws, t, 0, 4)
+            quantize_piece(wgs[t], wc, ws, t, 4, 8)
+            quantize_piece(wgs[t], wc, ws, t, 8, 9)
+
+        w1gs = {}
+
+        def c_run(q, half):
+            if half == "a":
+                w1g_new = stage.tile([P, NK * 512], BF16, name="w1g", tag="grouped", align_bytes=64)
+                w1gs[q] = w1g_new
+            w1g = w1gs[q]
             words = w1raw[q][:].bitcast(F32).rearrange("m (k a u) -> m k u a", k=NK, u=2)
-            for k0 in range(0, NK, 2):
-                nk = min(2, NK - k0)
+            for k0, nk in C_RUNS[half]:
                 tp1 = work.tile([P, 2, 2, P], F32, name="tp1", tag="bank")
                 for kk in range(nk):
                     for u in range(2):
@@ -134,14 +148,14 @@ def tile_psr4convf_kernel(tc, x, W, W1, out):
                     .rearrange("p (k m u) -> p k m u", k=nk, u=2)
                 )
                 nc.scalar.copy(out=dst, in_=tp1[:, 0:nk, :, :].rearrange("p k u m -> p k m u"))
-                if k0 == 4:
-                    quantize_piece(w1g, w1c, w1s, q, 0, 4)
-                if k0 == 8:
-                    quantize_piece(w1g, w1c, w1s, q, 4, 8)
-            quantize_piece(w1g, w1c, w1s, q, 8, 9)
+            for k0, k1 in C_PIECES[half]:
+                quantize_piece(w1g, w1c, w1s, q, k0, k1)
+
+        set_of = {}
 
         def stage1(k):
-            h0, hp, hm = hset[k % NSET]
+            set_of[k] = hset[len(set_of) % NSET]
+            h0, hp, hm = set_of[k]
             h0f = h0[:].rearrange("p a b t -> p (a b t)")
             for nh in range(2):
                 z = work.tile([P, 4, P], Z_DT, name="z", tag="bank")
@@ -169,9 +183,9 @@ def tile_psr4convf_kernel(tc, x, W, W1, out):
                     nc.vector.tensor_copy(out=hm[:, 1:17, 1:16, :], in_=h0[:, 1:17, 0:15, :])
 
         def versions(k):
-            h0, hp, hm = hset[k % NSET]
+            h0, hp, hm = set_of[k]
             by_dx = {0: h0, 1: hp, -1: hm}
-            for v in range(4 if k < 8 else 2):
+            for v in range(4 if k < 8 else 1):
                 dy, dx = RING[(k + 2 * v) % 8] if k < 8 else (0, 0)
                 flat = by_dx[dx][:].rearrange("p a b t -> p (a b t)")
                 nc.vector.quantize_mx(
@@ -180,72 +194,127 @@ def tile_psr4convf_kernel(tc, x, W, W1, out):
                     in_=flat[:, (1 + dy) * ROW : (1 + dy) * ROW + 4 * HW],
                 )
 
+        centre = {}
+
+        def centre_term(q):
+            c0 = (q * NK + 8) * P
+            ups = work.tile([P, HW], F32, name="ups", tag="bank")
+            nc.tensor.matmul_mx(
+                out=ups[:],
+                lhsT=w1c[:, c0 : c0 + P].bitcast(FP8X4),
+                lhsT_scale=w1s[:, c0 : c0 + P],
+                rhs=hc[8][:].bitcast(FP8X4),
+                rhs_scale=hs[8][:],
+                start=True,
+                stop=True,
+            )
+            u8 = const.tile([P, 2, HW], F32, name="u8_%d" % q)
+            nc.scalar.copy(out=u8[:, 0, :], in_=ups[:])
+            nc.scalar.copy(out=u8[:, 1, :], in_=ups[:])
+            centre[q] = u8
+
         accs = {}
 
         def open_group(q, rp):
             acc = accp.tile([P, 512], F32, name="acc", tag="acc")
             accs[(q, rp)] = acc
 
-        def stage2(q, rp, k, first_pass, last_pass):
+        def stage2(q, rp, k):
             c0 = (q * NK + k) * P
-            r0 = rp * 512 if k < 8 else 0
             nc.tensor.matmul_mx(
                 out=accs[(q, rp)][:],
                 lhsT=w1c[:, c0 : c0 + P].bitcast(FP8X4),
                 lhsT_scale=w1s[:, c0 : c0 + P],
-                rhs=hc[k][:, r0 : r0 + 512].bitcast(FP8X4),
-                rhs_scale=hs[k][:, r0 : r0 + 512],
-                start=first_pass,
-                stop=last_pass,
+                rhs=hc[k][:, rp * 512 : (rp + 1) * 512].bitcast(FP8X4),
+                rhs_scale=hs[k][:, rp * 512 : (rp + 1) * 512],
+                start=(k == 0),
+                stop=(k == 7),
             )
 
         def finish_group(q, rp):
             osb = outp.tile([P, 512], F32, name="osb", tag="osb")
-            if rp == 0:
-                nc.vector.tensor_copy(out=osb[:], in_=accs[(q, rp)][:])
-            else:
-                nc.scalar.copy(out=osb[:], in_=accs[(q, rp)][:])
+            nc.vector.tensor_tensor(
+                out=osb[:], in0=accs[(q, rp)][:], in1=centre[q][:].rearrange("p r n -> p (r n)"), op=ADD
+            )
             nc.sync.dma_start(out=out_v[:, q, rp * 512 : (rp + 1) * 512], in_=osb[:])
 
-        ks = [8, 0, 1, 2, 3, 4, 5, 6, 7]
         first = [(q, rp) for q in (0, 1) for rp in (0, 1)]
 
-        def whole_group(q, rp):
-            open_group(q, rp)
-            for k in range(NK):
-                stage2(q, rp, k, k == 0, k == NK - 1)
-            finish_group(q, rp)
+        def sweep(k):
+            for g in first:
+                stage2(g[0], g[1], k)
 
         with tc.manual_schedule(engines={mybir.EngineType.PE}):
-            wps = work.tile([P, 512], F32, name="wps", tag="bank")
-            for i in range(N_WARM):
-                nc.tensor.matmul(out=wps[:], lhsT=dummy[:, 0:P], rhs=dummy[:], start=True, stop=True)
-            w_chunk(0)
+            burst(N_WARM, dummy[:, 0:P], dummy[:])
+            burst(2, wraw[0][:, 0:P], wraw[0][:, 0:512])
+            w_tiles(0)
+            load_w1(1)
+            w_tiles(1)
             load_w1(2)
-            w_chunk(1)
+            w_quant(0)
+            w_tiles(2)
             load_w1(3)
-            w_chunk(2)
-            w_chunk(3)
-            w1_chunk(0)
+            w_quant(1)
+            w_tiles(3)
+            x_prep()
+            w_quant(2)
+            w_quant(3)
+            c_run(0, "a")
+            burst(2, dummy[:, 0:P], dummy[:])
+            c_run(0, "b")
+            burst(2, dummy[:, 0:P], dummy[:])
+            c_run(1, "a")
             for g in first:
                 open_group(g[0], g[1])
-            for s in range(NK):
-                stage1(ks[s])
-                if s >= 1:
-                    versions(ks[s - 1])
-                if s == 1:
-                    w1_chunk(1)
-                if s >= 2:
-                    for g in first:
-                        stage2(g[0], g[1], ks[s - 2], s == 2, False)
-            versions(ks[NK - 1])
-            w1_chunk(2)
+            stage1(8)
+            stage1(0)
+            c_run(1, "b")
+            versions(8)
+            stage1(1)
+            versions(0)
+            centre_term(0)
+            centre_term(1)
+            stage1(2)
+            versions(1)
+            sweep(0)
+            c_run(2, "a")
+            stage1(3)
+            versions(2)
+            sweep(1)
+            stage1(4)
+            versions(3)
+            sweep(2)
+            stage1(5)
+            versions(4)
+            sweep(3)
+            stage1(6)
+            versions(5)
+            sweep(4)
+            stage1(7)
+            versions(6)
+            sweep(5)
+            versions(7)
+            c_run(2, "b")
+            sweep(6)
+            centre_term(2)
             for g in first:
-                stage2(g[0], g[1], ks[NK - 2], False, False)
-                stage2(g[0], g[1], ks[NK - 1], False, True)
+                stage2(g[0], g[1], 7)
                 finish_group(g[0], g[1])
-            whole_group(2, 0)
-            w1_chunk(3)
-            whole_group(2, 1)
-            whole_group(3, 0)
-            whole_group(3, 1)
+            open_group(2, 0)
+            for k in range(8):
+                stage2(2, 0, k)
+            finish_group(2, 0)
+            c_run(3, "a")
+            open_group(2, 1)
+            for k in range(4):
+                stage2(2, 1, k)
+            c_run(3, "b")
+            for k in range(4, 8):
+                stage2(2, 1, k)
+            finish_group(2, 1)
+            centre_term(3)
+            for rp in range(2):
+                open_group(3, rp)
+                for k in range(8):
+                    stage2(3, rp, k)
+                finish_group(3, rp)

@@ -9,7 +9,6 @@ U32 = mybir.dt.uint32
 U8 = mybir.dt.uint8
 FP8X4 = mybir.dt.float8_e4m3fn_x4
 RELU = mybir.ActivationFunctionType.Relu
-ADD = mybir.AluOpType.add
 
 P = 128
 NK = 9
@@ -17,10 +16,9 @@ HW = 256
 ROW = 64
 RING = [(-1, -1), (-1, 0), (-1, 1), (0, 1), (1, 1), (1, 0), (1, -1), (0, -1)]
 NSET = 3
-N_WARM = 6
+N_WARM = 8
 Z_DT = F32
-C_RUNS = {"a": [(0, 2), (2, 2), (4, 1)], "b": [(5, 2), (7, 2)]}
-C_PIECES = {"a": [(0, 4), (4, 5)], "b": [(5, 9)]}
+C_TILES = [(0, 2), (2, 2), (4, 2), (6, 2), (8, 1)]
 
 FLOPS = 2 * 2 * NK * 512 * 512 * HW
 
@@ -37,8 +35,7 @@ def tile_psr4convf_kernel(tc, x, W, W1, out):
         raw = ctx.enter_context(tc.tile_pool(name="raw", bufs=5))
         stage = ctx.enter_context(tc.tile_pool(name="stage", bufs=5))
         outp = ctx.enter_context(tc.tile_pool(name="outp", bufs=4))
-        work = ctx.enter_context(tc.psum_pool(name="work", bufs=4))
-        accp = ctx.enter_context(tc.psum_pool(name="accp", bufs=4))
+        work = ctx.enter_context(tc.psum_pool(name="work", bufs=8))
 
         wraw = []
         for t in range(4):
@@ -62,14 +59,19 @@ def tile_psr4convf_kernel(tc, x, W, W1, out):
         make_identity(nc, ident_bf[:])
         ident_f = const.tile([P, P], F32, name="ident_f")
         make_identity(nc, ident_f[:])
+        h0s = []
+        for k in range(NK):
+            h0k = const.tile([P, 18, 16, 4], BF16, name="h0_%d" % k, align_bytes=64)
+            nc.vector.memset(h0k[:, 0:18:17, :, :], 0.0)
+            h0s.append(h0k)
         hset = []
         for s in range(NSET):
-            trio = []
-            for nm in ("h0", "hp", "hm"):
+            pair = []
+            for nm in ("hp", "hm"):
                 ht = const.tile([P, 18, 16, 4], BF16, name="%s_%d" % (nm, s), align_bytes=64)
                 nc.vector.memset(ht[:], 0.0)
-                trio.append(ht)
-            hset.append(trio)
+                pair.append(ht)
+            hset.append(pair)
         warm = const.tile([P, 1], F32, name="warm")
         nc.vector.memset(warm[:], 0.0)
         nc.scalar.activation(out=warm[:], in_=warm[:], func=RELU)
@@ -84,7 +86,7 @@ def tile_psr4convf_kernel(tc, x, W, W1, out):
         hc = []
         hs = []
         for k in range(NK):
-            nver = 4 if k < 8 else 1
+            nver = 4 if k < 8 else 2
             hck = const.tile([P, nver * HW], U32, name="hc%d" % k, align_bytes=64)
             hsk = const.tile([P, nver * HW], U8, name="hs%d" % k, align_bytes=64)
             hc.append(hck)
@@ -129,15 +131,10 @@ def tile_psr4convf_kernel(tc, x, W, W1, out):
             quantize_piece(wgs[t], wc, ws, t, 4, 8)
             quantize_piece(wgs[t], wc, ws, t, 8, 9)
 
-        w1gs = {}
-
-        def c_run(q, half):
-            if half == "a":
-                w1g_new = stage.tile([P, NK * 512], BF16, name="w1g", tag="grouped", align_bytes=64)
-                w1gs[q] = w1g_new
-            w1g = w1gs[q]
+        def c_run(q):
+            w1g = stage.tile([P, NK * 512], BF16, name="w1g", tag="grouped", align_bytes=64)
             words = w1raw[q][:].bitcast(F32).rearrange("m (k a u) -> m k u a", k=NK, u=2)
-            for k0, nk in C_RUNS[half]:
+            for k0, nk in C_TILES:
                 tp1 = work.tile([P, 2, 2, P], F32, name="tp1", tag="bank")
                 for kk in range(nk):
                     for u in range(2):
@@ -148,14 +145,18 @@ def tile_psr4convf_kernel(tc, x, W, W1, out):
                     .rearrange("p (k m u) -> p k m u", k=nk, u=2)
                 )
                 nc.scalar.copy(out=dst, in_=tp1[:, 0:nk, :, :].rearrange("p k u m -> p k m u"))
-            for k0, k1 in C_PIECES[half]:
-                quantize_piece(w1g, w1c, w1s, q, k0, k1)
+                if k0 == 2:
+                    quantize_piece(w1g, w1c, w1s, q, 0, 4)
+                if k0 == 6:
+                    quantize_piece(w1g, w1c, w1s, q, 4, 8)
+            quantize_piece(w1g, w1c, w1s, q, 8, 9)
 
         set_of = {}
 
         def stage1(k):
-            set_of[k] = hset[len(set_of) % NSET]
-            h0, hp, hm = set_of[k]
+            set_of[k] = hset[k % NSET]
+            h0 = h0s[k]
+            hp, hm = set_of[k]
             h0f = h0[:].rearrange("p a b t -> p (a b t)")
             for nh in range(2):
                 z = work.tile([P, 4, P], Z_DT, name="z", tag="bank")
@@ -177,15 +178,13 @@ def tile_psr4convf_kernel(tc, x, W, W1, out):
                 )
             if k < 8:
                 nc.vector.tensor_copy(out=hp[:, 1:17, 0:15, :], in_=h0[:, 1:17, 1:16, :])
-                if k % 2 == 1:
-                    nc.scalar.copy(out=hm[:, 1:17, 1:16, :], in_=h0[:, 1:17, 0:15, :])
-                else:
-                    nc.vector.tensor_copy(out=hm[:, 1:17, 1:16, :], in_=h0[:, 1:17, 0:15, :])
+                nc.vector.tensor_copy(out=hm[:, 1:17, 1:16, :], in_=h0[:, 1:17, 0:15, :])
 
-        def versions(k):
-            h0, hp, hm = set_of[k]
+        def versions(k, which):
+            h0 = h0s[k]
+            hp, hm = set_of[k]
             by_dx = {0: h0, 1: hp, -1: hm}
-            for v in range(4 if k < 8 else 1):
+            for v in which:
                 dy, dx = RING[(k + 2 * v) % 8] if k < 8 else (0, 0)
                 flat = by_dx[dx][:].rearrange("p a b t -> p (a b t)")
                 nc.vector.quantize_mx(
@@ -194,127 +193,91 @@ def tile_psr4convf_kernel(tc, x, W, W1, out):
                     in_=flat[:, (1 + dy) * ROW : (1 + dy) * ROW + 4 * HW],
                 )
 
-        centre = {}
-
-        def centre_term(q):
-            c0 = (q * NK + 8) * P
-            ups = work.tile([P, HW], F32, name="ups", tag="bank")
-            nc.tensor.matmul_mx(
-                out=ups[:],
-                lhsT=w1c[:, c0 : c0 + P].bitcast(FP8X4),
-                lhsT_scale=w1s[:, c0 : c0 + P],
-                rhs=hc[8][:].bitcast(FP8X4),
-                rhs_scale=hs[8][:],
-                start=True,
-                stop=True,
-            )
-            u8 = const.tile([P, 2, HW], F32, name="u8_%d" % q)
-            nc.scalar.copy(out=u8[:, 0, :], in_=ups[:])
-            nc.scalar.copy(out=u8[:, 1, :], in_=ups[:])
-            centre[q] = u8
-
         accs = {}
 
         def open_group(q, rp):
-            acc = accp.tile([P, 512], F32, name="acc", tag="acc")
+            acc = work.tile([P, 512], F32, name="acc", tag="bank")
             accs[(q, rp)] = acc
 
-        def stage2(q, rp, k):
+        def stage2(q, rp, k, first_pass, last_pass):
             c0 = (q * NK + k) * P
+            r0 = rp * 512 if k < 8 else 0
             nc.tensor.matmul_mx(
                 out=accs[(q, rp)][:],
                 lhsT=w1c[:, c0 : c0 + P].bitcast(FP8X4),
                 lhsT_scale=w1s[:, c0 : c0 + P],
-                rhs=hc[k][:, rp * 512 : (rp + 1) * 512].bitcast(FP8X4),
-                rhs_scale=hs[k][:, rp * 512 : (rp + 1) * 512],
-                start=(k == 0),
-                stop=(k == 7),
+                rhs=hc[k][:, r0 : r0 + 512].bitcast(FP8X4),
+                rhs_scale=hs[k][:, r0 : r0 + 512],
+                start=first_pass,
+                stop=last_pass,
             )
 
         def finish_group(q, rp):
             osb = outp.tile([P, 512], F32, name="osb", tag="osb")
-            nc.vector.tensor_tensor(
-                out=osb[:], in0=accs[(q, rp)][:], in1=centre[q][:].rearrange("p r n -> p (r n)"), op=ADD
-            )
+            if q % 2 == 0:
+                nc.vector.tensor_copy(out=osb[:], in_=accs[(q, rp)][:])
+            else:
+                nc.scalar.copy(out=osb[:], in_=accs[(q, rp)][:])
             nc.sync.dma_start(out=out_v[:, q, rp * 512 : (rp + 1) * 512], in_=osb[:])
 
-        first = [(q, rp) for q in (0, 1) for rp in (0, 1)]
+        g01 = [(q, rp) for q in (0, 1) for rp in (0, 1)]
+        g23 = [(q, rp) for q in (2, 3) for rp in (0, 1)]
 
-        def sweep(k):
-            for g in first:
-                stage2(g[0], g[1], k)
+        def sweep(groups, k):
+            for g in groups:
+                stage2(g[0], g[1], k, k == 0, k == 7)
 
         with tc.manual_schedule(engines={mybir.EngineType.PE}):
             burst(N_WARM, dummy[:, 0:P], dummy[:])
-            burst(2, wraw[0][:, 0:P], wraw[0][:, 0:512])
             w_tiles(0)
             load_w1(1)
             w_tiles(1)
             load_w1(2)
-            w_quant(0)
             w_tiles(2)
             load_w1(3)
-            w_quant(1)
             w_tiles(3)
             x_prep()
-            w_quant(2)
-            w_quant(3)
-            c_run(0, "a")
-            burst(2, dummy[:, 0:P], dummy[:])
-            c_run(0, "b")
-            burst(2, dummy[:, 0:P], dummy[:])
-            c_run(1, "a")
-            for g in first:
-                open_group(g[0], g[1])
-            stage1(8)
+            for t in range(4):
+                w_quant(t)
+            c_run(0)
+            c_run(1)
             stage1(0)
-            c_run(1, "b")
-            versions(8)
             stage1(1)
-            versions(0)
-            centre_term(0)
-            centre_term(1)
+            versions(0, (0, 1, 2, 3))
+            c_run(2)
+            versions(1, (0, 1, 2, 3))
             stage1(2)
-            versions(1)
-            sweep(0)
-            c_run(2, "a")
             stage1(3)
-            versions(2)
-            sweep(1)
+            versions(2, (0, 1, 2, 3))
+            c_run(3)
+            versions(3, (0, 1, 2, 3))
+            for g in g01:
+                open_group(g[0], g[1])
+            sweep(g01, 0)
+            sweep(g01, 1)
             stage1(4)
-            versions(3)
-            sweep(2)
             stage1(5)
-            versions(4)
-            sweep(3)
+            versions(4, (0, 1, 2, 3))
+            sweep(g01, 2)
             stage1(6)
-            versions(5)
-            sweep(4)
             stage1(7)
-            versions(6)
-            sweep(5)
-            versions(7)
-            c_run(2, "b")
-            sweep(6)
-            centre_term(2)
-            for g in first:
-                stage2(g[0], g[1], 7)
-                finish_group(g[0], g[1])
-            open_group(2, 0)
-            for k in range(8):
-                stage2(2, 0, k)
-            finish_group(2, 0)
-            c_run(3, "a")
-            open_group(2, 1)
+            versions(5, (0, 1, 2, 3))
+            sweep(g01, 3)
+            stage1(8)
+            for g in g23:
+                open_group(g[0], g[1])
             for k in range(4):
-                stage2(2, 1, k)
-            c_run(3, "b")
-            for k in range(4, 8):
-                stage2(2, 1, k)
-            finish_group(2, 1)
-            centre_term(3)
+                sweep(g23, k)
+            versions(8, (0, 1))
+            versions(6, (0, 1))
+            versions(7, (0, 1))
+            sweep(g01 + g23, 4)
+            versions(6, (2, 3))
+            versions(7, (2, 3))
+            sweep(g01 + g23, 5)
+            sweep(g01 + g23, 8)
             for rp in range(2):
-                open_group(3, rp)
-                for k in range(8):
-                    stage2(3, rp, k)
-                finish_group(3, rp)
+                for q in range(4):
+                    stage2(q, rp, 6, False, False)
+                    stage2(q, rp, 7, False, True)
+                    finish_group(q, rp)

@@ -16,6 +16,7 @@ HW = 256
 ROW = 64
 RING = [(-1, -1), (-1, 0), (-1, 1), (0, 1), (1, 1), (1, 0), (1, -1), (0, -1)]
 NSET = 3
+N_H0 = 5
 N_WARM = 8
 Z_DT = F32
 C_TILES = [(0, 2), (2, 2), (4, 2), (6, 2), (8, 1)]
@@ -32,7 +33,8 @@ def tile_psr4convf_kernel(tc, x, W, W1, out):
 
     with ExitStack() as ctx:
         const = ctx.enter_context(tc.tile_pool(name="const", bufs=1))
-        raw = ctx.enter_context(tc.tile_pool(name="raw", bufs=5))
+        raw = ctx.enter_context(tc.tile_pool(name="raw", bufs=4))
+        regr = ctx.enter_context(tc.tile_pool(name="regr", bufs=2))
         stage = ctx.enter_context(tc.tile_pool(name="stage", bufs=5))
         outp = ctx.enter_context(tc.tile_pool(name="outp", bufs=4))
         work = ctx.enter_context(tc.psum_pool(name="work", bufs=8))
@@ -51,16 +53,12 @@ def tile_psr4convf_kernel(tc, x, W, W1, out):
             nc.sync.dma_start(out=r1[:], in_=w1_v[:, q, :])
             w1raw.append(r1)
 
-        load_w1(0)
-
         dummy = const.tile([P, 512], BF16, name="dummy")
         nc.vector.memset(dummy[:], 0.0)
-        ident_bf = const.tile([P, P], BF16, name="ident_bf")
-        make_identity(nc, ident_bf[:])
         ident_f = const.tile([P, P], F32, name="ident_f")
         make_identity(nc, ident_f[:])
         h0s = []
-        for k in range(NK):
+        for k in range(N_H0):
             h0k = const.tile([P, 18, 16, 4], BF16, name="h0_%d" % k, align_bytes=64)
             nc.vector.memset(h0k[:, 0:18:17, :, :], 0.0)
             h0s.append(h0k)
@@ -112,19 +110,31 @@ def tile_psr4convf_kernel(tc, x, W, W1, out):
 
         wgs = {}
 
+        def transposed(words, grouped):
+            for k0, nk in C_TILES:
+                tp1 = work.tile([P, 2, 2, P], F32, name="tp1", tag="bank")
+                for kk in range(nk):
+                    for u in range(2):
+                        nc.tensor.transpose(out=tp1[:, kk, u, :], in_=words[:, k0 + kk, u, :], identity=ident_f[:])
+                dst = (
+                    grouped[:, k0 * 512 : (k0 + nk) * 512]
+                    .bitcast(F32)
+                    .rearrange("p (k m u) -> p k m u", k=nk, u=2)
+                )
+                nc.scalar.copy(out=dst, in_=tp1[:, 0:nk, :, :].rearrange("p k u m -> p k m u"))
+
         def w_tiles(t):
+            wk = regr.tile([P, NK, 2, P, 2], BF16, name="wk", tag="wk")
+            src = wraw[t][:].rearrange("m (a u e k) -> m k u a e", u=2, e=2, k=NK)
+            for k0, k1 in ((0, 4), (4, 8)):
+                for u in range(2):
+                    nc.vector.tensor_copy(out=wk[:, k0:k1, u, :, :], in_=src[:, k0:k1, u, :, :])
+            for u in range(2):
+                nc.scalar.copy(out=wk[:, 8, u, :, :], in_=src[:, 8, u, :, :])
             wg = stage.tile([P, NK * 512], BF16, name="wg", tag="grouped", align_bytes=64)
             wgs[t] = wg
-            src = wraw[t][:].rearrange("m (a j k) -> m j k a", j=4, k=NK)
-            for k in range(NK):
-                tp = work.tile([P, 4, P], BF16, name="tpw", tag="bank")
-                for j in range(4):
-                    nc.tensor.transpose(out=tp[:, j, :], in_=src[:, j, k, :], identity=ident_bf[:])
-                dst = wg[:, k * 512 : (k + 1) * 512].rearrange("p (m j) -> p m j", j=4)
-                if k % 2 == 0:
-                    nc.scalar.copy(out=dst, in_=tp[:].rearrange("p j m -> p m j"))
-                else:
-                    nc.vector.tensor_copy(out=dst, in_=tp[:].rearrange("p j m -> p m j"))
+            words = wk[:].rearrange("m k u a e -> m (k u a e)").bitcast(F32).rearrange("m (k u a) -> m k u a", k=NK, u=2)
+            transposed(words, wg)
 
         def w_quant(t):
             quantize_piece(wgs[t], wc, ws, t, 0, 4)
@@ -155,7 +165,7 @@ def tile_psr4convf_kernel(tc, x, W, W1, out):
 
         def stage1(k):
             set_of[k] = hset[k % NSET]
-            h0 = h0s[k]
+            h0 = h0s[k % N_H0]
             hp, hm = set_of[k]
             h0f = h0[:].rearrange("p a b t -> p (a b t)")
             for nh in range(2):
@@ -181,7 +191,7 @@ def tile_psr4convf_kernel(tc, x, W, W1, out):
                 nc.vector.tensor_copy(out=hm[:, 1:17, 1:16, :], in_=h0[:, 1:17, 0:15, :])
 
         def versions(k, which):
-            h0 = h0s[k]
+            h0 = h0s[k % N_H0]
             hp, hm = set_of[k]
             by_dx = {0: h0, 1: hp, -1: hm}
             for v in which:
@@ -229,13 +239,9 @@ def tile_psr4convf_kernel(tc, x, W, W1, out):
 
         with tc.manual_schedule(engines={mybir.EngineType.PE}):
             burst(N_WARM, dummy[:, 0:P], dummy[:])
-            w_tiles(0)
-            load_w1(1)
-            w_tiles(1)
-            load_w1(2)
-            w_tiles(2)
-            load_w1(3)
-            w_tiles(3)
+            for t in range(4):
+                w_tiles(t)
+                load_w1(t)
             x_prep()
             for t in range(4):
                 w_quant(t)

from contextlib import ExitStack

import concourse.mybir as mybir
from concourse.masks import make_identity

F32 = mybir.dt.float32
BF16 = mybir.dt.bfloat16
U32 = mybir.dt.uint32
U8 = mybir.dt.uint8
FP8X4 = mybir.dt.float8_e4m3fn_x4
RELU = mybir.ActivationFunctionType.Relu

P = 128
NK = 9
HW = 256
ROW = 64
RING = [(-1, -1), (-1, 0), (-1, 1), (0, 1), (1, 1), (1, 0), (1, -1), (0, -1)]
NSET = 3
N_H0 = 5
N_WARM = 8
Z_DT = F32
C_TILES = [(0, 2), (2, 2), (4, 2), (6, 2), (8, 1)]

FLOPS = 2 * 2 * NK * 512 * 512 * HW


def tile_psr4convf_kernel(tc, x, W, W1, out):
    nc = tc.nc
    x_v = x[0].rearrange("(p j) h w -> p j (h w)", j=4)
    w_v = W.rearrange("(m t) c k -> m t (c k)", t=4)
    w1_v = W1.rearrange("(m q) f -> m q f", q=4)
    out_v = out[0].rearrange("(m q) r h w -> m q (r h w)", q=4)

    with ExitStack() as ctx:
        const = ctx.enter_context(tc.tile_pool(name="const", bufs=1))
        raw = ctx.enter_context(tc.tile_pool(name="raw", bufs=4))
        regr = ctx.enter_context(tc.tile_pool(name="regr", bufs=2))
        stage = ctx.enter_context(tc.tile_pool(name="stage", bufs=5))
        outp = ctx.enter_context(tc.tile_pool(name="outp", bufs=4))
        work = ctx.enter_context(tc.psum_pool(name="work", bufs=8))

        wraw = []
        for t in range(4):
            r = raw.tile([P, NK * 512], BF16, name="wraw%d" % t, tag="raw")
            nc.sync.dma_start(out=r[:], in_=w_v[:, t, :])
            wraw.append(r)
        xraw = const.tile([P, 4, HW], BF16, name="xraw")
        nc.sync.dma_start(out=xraw[:], in_=x_v)
        w1raw = []

        def load_w1(q):
            r1 = raw.tile([P, NK * 512], BF16, name="w1raw%d" % q, tag="raw")
            nc.sync.dma_start(out=r1[:], in_=w1_v[:, q, :])
            w1raw.append(r1)

        dummy = const.tile([P, 512], BF16, name="dummy")
        nc.vector.memset(dummy[:], 0.0)
        ident_f = const.tile([P, P], F32, name="ident_f")
        make_identity(nc, ident_f[:])
        h0s = []
        for k in range(N_H0):
            h0k = const.tile([P, 18, 16, 4], BF16, name="h0_%d" % k, align_bytes=64)
            nc.vector.memset(h0k[:, 0:18:17, :, :], 0.0)
            h0s.append(h0k)
        hset = []
        for s in range(NSET):
            pair = []
            for nm in ("hp", "hm"):
                ht = const.tile([P, 18, 16, 4], BF16, name="%s_%d" % (nm, s), align_bytes=64)
                nc.vector.memset(ht[:], 0.0)
                pair.append(ht)
            hset.append(pair)
        warm = const.tile([P, 1], F32, name="warm")
        nc.vector.memset(warm[:], 0.0)
        nc.scalar.activation(out=warm[:], in_=warm[:], func=RELU)

        xg = const.tile([P, HW, 4], BF16, name="xg", align_bytes=64)
        xc = const.tile([P, HW], U32, name="xc", align_bytes=64)
        xs = const.tile([P, HW], U8, name="xs", align_bytes=64)
        wc = const.tile([P, 4 * NK * P], U32, name="wc", align_bytes=64)
        ws = const.tile([P, 4 * NK * P], U8, name="ws", align_bytes=64)
        w1c = const.tile([P, 4 * NK * P], U32, name="w1c", align_bytes=64)
        w1s = const.tile([P, 4 * NK * P], U8, name="w1s", align_bytes=64)
        hc = []
        hs = []
        for k in range(NK):
            nver = 4 if k < 8 else 2
            hck = const.tile([P, nver * HW], U32, name="hc%d" % k, align_bytes=64)
            hsk = const.tile([P, nver * HW], U8, name="hs%d" % k, align_bytes=64)
            hc.append(hck)
            hs.append(hsk)

        def x_prep():
            nc.vector.tensor_copy(out=xg[:], in_=xraw[:].rearrange("p j n -> p n j"))
            nc.vector.quantize_mx(out=xc[:].bitcast(FP8X4), scales=xs[:], in_=xg[:].rearrange("p n j -> p (n j)"))

        def quantize_piece(grouped, codes, scales, chunk, k0, k1):
            c0 = (chunk * NK + k0) * P
            c1 = (chunk * NK + k1) * P
            nc.vector.quantize_mx(
                out=codes[:, c0:c1].bitcast(FP8X4),
                scales=scales[:, c0:c1],
                in_=grouped[:, k0 * 512 : k1 * 512],
            )

        def burst(n, lhs, rhs):
            wps = work.tile([P, 512], F32, name="wps", tag="bank")
            for i in range(n):
                nc.tensor.matmul(out=wps[:], lhsT=lhs, rhs=rhs, start=True, stop=True)

        wgs = {}

        def transposed(words, grouped):
            for k0, nk in C_TILES:
                tp1 = work.tile([P, 2, 2, P], F32, name="tp1", tag="bank")
                for kk in range(nk):
                    for u in range(2):
                        nc.tensor.transpose(out=tp1[:, kk, u, :], in_=words[:, k0 + kk, u, :], identity=ident_f[:])
                dst = (
                    grouped[:, k0 * 512 : (k0 + nk) * 512]
                    .bitcast(F32)
                    .rearrange("p (k m u) -> p k m u", k=nk, u=2)
                )
                nc.scalar.copy(out=dst, in_=tp1[:, 0:nk, :, :].rearrange("p k u m -> p k m u"))

        def w_tiles(t):
            wk = regr.tile([P, NK, 2, P, 2], BF16, name="wk", tag="wk")
            src = wraw[t][:].rearrange("m (a u e k) -> m k u a e", u=2, e=2, k=NK)
            for k0, k1 in ((0, 4), (4, 8)):
                for u in range(2):
                    nc.vector.tensor_copy(out=wk[:, k0:k1, u, :, :], in_=src[:, k0:k1, u, :, :])
            for u in range(2):
                nc.scalar.copy(out=wk[:, 8, u, :, :], in_=src[:, 8, u, :, :])
            wg = stage.tile([P, NK * 512], BF16, name="wg", tag="grouped", align_bytes=64)
            wgs[t] = wg
            words = wk[:].rearrange("m k u a e -> m (k u a e)").bitcast(F32).rearrange("m (k u a) -> m k u a", k=NK, u=2)
            transposed(words, wg)

        def w_quant(t):
            quantize_piece(wgs[t], wc, ws, t, 0, 4)
            quantize_piece(wgs[t], wc, ws, t, 4, 8)
            quantize_piece(wgs[t], wc, ws, t, 8, 9)

        def c_run(q):
            w1g = stage.tile([P, NK * 512], BF16, name="w1g", tag="grouped", align_bytes=64)
            words = w1raw[q][:].bitcast(F32).rearrange("m (k a u) -> m k u a", k=NK, u=2)
            for k0, nk in C_TILES:
                tp1 = work.tile([P, 2, 2, P], F32, name="tp1", tag="bank")
                for kk in range(nk):
                    for u in range(2):
                        nc.tensor.transpose(out=tp1[:, kk, u, :], in_=words[:, k0 + kk, u, :], identity=ident_f[:])
                dst = (
                    w1g[:, k0 * 512 : (k0 + nk) * 512]
                    .bitcast(F32)
                    .rearrange("p (k m u) -> p k m u", k=nk, u=2)
                )
                nc.scalar.copy(out=dst, in_=tp1[:, 0:nk, :, :].rearrange("p k u m -> p k m u"))
                if k0 == 2:
                    quantize_piece(w1g, w1c, w1s, q, 0, 4)
                if k0 == 6:
                    quantize_piece(w1g, w1c, w1s, q, 4, 8)
            quantize_piece(w1g, w1c, w1s, q, 8, 9)

        set_of = {}

        def stage1(k):
            set_of[k] = hset[k % NSET]
            h0 = h0s[k % N_H0]
            hp, hm = set_of[k]
            h0f = h0[:].rearrange("p a b t -> p (a b t)")
            for nh in range(2):
                z = work.tile([P, 4, P], Z_DT, name="z", tag="bank")
                for t in range(4):
                    c0 = (t * NK + k) * P
                    nc.tensor.matmul_mx(
                        out=z[:, t, :],
                        lhsT=wc[:, c0 : c0 + P].bitcast(FP8X4),
                        lhsT_scale=ws[:, c0 : c0 + P],
                        rhs=xc[:, nh * P : (nh + 1) * P].bitcast(FP8X4),
                        rhs_scale=xs[:, nh * P : (nh + 1) * P],
                        start=True,
                        stop=True,
                    )
                nc.scalar.activation(
                    out=h0f[:, ROW + nh * 512 : ROW + (nh + 1) * 512].rearrange("p (n t) -> p n t", t=4),
                    in_=z[:].rearrange("p t n -> p n t"),
                    func=RELU,
                )
            if k < 8:
                nc.vector.tensor_copy(out=hp[:, 1:17, 0:15, :], in_=h0[:, 1:17, 1:16, :])
                nc.vector.tensor_copy(out=hm[:, 1:17, 1:16, :], in_=h0[:, 1:17, 0:15, :])

        def versions(k, which):
            h0 = h0s[k % N_H0]
            hp, hm = set_of[k]
            by_dx = {0: h0, 1: hp, -1: hm}
            for v in which:
                dy, dx = RING[(k + 2 * v) % 8] if k < 8 else (0, 0)
                flat = by_dx[dx][:].rearrange("p a b t -> p (a b t)")
                nc.vector.quantize_mx(
                    out=hc[k][:, v * HW : (v + 1) * HW].bitcast(FP8X4),
                    scales=hs[k][:, v * HW : (v + 1) * HW],
                    in_=flat[:, (1 + dy) * ROW : (1 + dy) * ROW + 4 * HW],
                )

        accs = {}

        def open_group(q, rp):
            acc = work.tile([P, 512], F32, name="acc", tag="bank")
            accs[(q, rp)] = acc

        def stage2(q, rp, k, first_pass, last_pass):
            c0 = (q * NK + k) * P
            r0 = rp * 512 if k < 8 else 0
            nc.tensor.matmul_mx(
                out=accs[(q, rp)][:],
                lhsT=w1c[:, c0 : c0 + P].bitcast(FP8X4),
                lhsT_scale=w1s[:, c0 : c0 + P],
                rhs=hc[k][:, r0 : r0 + 512].bitcast(FP8X4),
                rhs_scale=hs[k][:, r0 : r0 + 512],
                start=first_pass,
                stop=last_pass,
            )

        def finish_group(q, rp):
            osb = outp.tile([P, 512], F32, name="osb", tag="osb")
            if q % 2 == 0:
                nc.vector.tensor_copy(out=osb[:], in_=accs[(q, rp)][:])
            else:
                nc.scalar.copy(out=osb[:], in_=accs[(q, rp)][:])
            nc.sync.dma_start(out=out_v[:, q, rp * 512 : (rp + 1) * 512], in_=osb[:])

        g01 = [(q, rp) for q in (0, 1) for rp in (0, 1)]
        g23 = [(q, rp) for q in (2, 3) for rp in (0, 1)]

        def sweep(groups, k):
            for g in groups:
                stage2(g[0], g[1], k, k == 0, k == 7)

        with tc.manual_schedule(engines={mybir.EngineType.PE}):
            burst(N_WARM, dummy[:, 0:P], dummy[:])
            for t in range(4):
                w_tiles(t)
                load_w1(t)
            x_prep()
            for t in range(4):
                w_quant(t)
            c_run(0)
            c_run(1)
            stage1(0)
            stage1(1)
            versions(0, (0, 1, 2, 3))
            c_run(2)
            versions(1, (0, 1, 2, 3))
            stage1(2)
            stage1(3)
            versions(2, (0, 1, 2, 3))
            c_run(3)
            versions(3, (0, 1, 2, 3))
            for g in g01:
                open_group(g[0], g[1])
            sweep(g01, 0)
            sweep(g01, 1)
            stage1(4)
            stage1(5)
            versions(4, (0, 1, 2, 3))
            sweep(g01, 2)
            stage1(6)
            stage1(7)
            versions(5, (0, 1, 2, 3))
            sweep(g01, 3)
            stage1(8)
            for g in g23:
                open_group(g[0], g[1])
            for k in range(4):
                sweep(g23, k)
            versions(8, (0, 1))
            versions(6, (0, 1))
            versions(7, (0, 1))
            sweep(g01 + g23, 4)
            versions(6, (2, 3))
            versions(7, (2, 3))
            sweep(g01 + g23, 5)
            sweep(g01 + g23, 8)
            for rp in range(2):
                for q in range(4):
                    stage2(q, rp, 6, False, False)
                    stage2(q, rp, 7, False, True)
                    finish_group(q, rp)
